import numpy as np
import ml_dtypes


def mxq(x, axis, fmt="e4m3"):
    dtype, down = {"e4m3": (ml_dtypes.float8_e4m3fn, 7), "e5m2": (ml_dtypes.float8_e5m2, 14)}[fmt]
    v = np.moveaxis(np.asarray(x, np.float32).astype(ml_dtypes.bfloat16).astype(np.float64), axis, -1)
    blocks = v.reshape(v.shape[:-1] + (-1, 32))
    amax = np.abs(blocks).max(-1, keepdims=True)
    byte = np.maximum(np.where(amax > 0, np.frexp(amax)[1] - 1 + 127, 0) - down, 1)
    scale = np.exp2(byte - 127.0)
    codes = (blocks / scale).astype(np.float32).astype(dtype).astype(np.float64)
    return np.moveaxis((codes * scale).reshape(v.shape), -1, axis)


WIDE = False


def mx_kscale(k):
    if not WIDE:
        return np.ones(k)
    levels = np.array([10, -10, 5, -5, 0])
    a = np.random.permutation(np.resize(levels, k // 512 * 4)).reshape(k // 512, 4)
    idx = np.arange(k)
    return np.exp2(a[idx // 512, idx % 128 // 32])


BF16 = ml_dtypes.bfloat16


def bf(x):
    return np.asarray(x, np.float32).astype(BF16)


def f64(x):
    return np.asarray(x).astype(np.float64)


B, N, E, H, NOPE, VDIM, ROPE, QR, KVR = 4, 1024, 1024, 4, 64, 128, 32, 512, 512
QH = NOPE + ROPE
BASE = 10000.0


def rope(v):
    d = v.shape[-1]
    n = v.shape[-2]
    theta = BASE ** (-2.0 * np.arange(d // 2) / d)
    ang = np.arange(n)[:, None] * theta[None, :]
    cos, sin = np.cos(ang), np.sin(ang)
    v1, v2 = v[..., 0::2], v[..., 1::2]
    return np.stack([v1 * cos - v2 * sin, v1 * sin + v2 * cos], axis=-1).reshape(v.shape)


def setup_inputs():
    s, t = mx_kscale(E), mx_kscale(QR)
    return {"x": bf(np.random.standard_normal((B, N, E)) * s),
            "Wqa": bf(np.random.standard_normal((E, QR)) / np.sqrt(E) / s[:, None] * t),
            "Wqb": bf(np.random.standard_normal((QR, H * QH)) / np.sqrt(QR) / t[:, None])}


def reference(x, Wqa, Wqb):
    cq = mxq(f64(x), 2, "e4m3") @ mxq(f64(Wqa), 0, "e4m3")
    q = mxq(cq, 2, "e4m3") @ mxq(f64(Wqb), 0, "e4m3")
    q = q.reshape(B, N, H, QH).transpose(0, 2, 1, 3)
    return np.concatenate([q[..., :NOPE], rope(q[..., NOPE:])], axis=-1)

@@ -1,0 +1,300 @@
+import math
+from contextlib import ExitStack
+
+import concourse.mybir as mybir
+from concourse.masks import make_identity
+
+F32 = mybir.dt.float32
+BF16 = mybir.dt.bfloat16
+I32 = mybir.dt.int32
+U32 = mybir.dt.uint32
+U8 = mybir.dt.uint8
+FP8X4 = mybir.dt.float8_e4m3fn_x4
+ALU = mybir.AluOpType
+ACT = mybir.ActivationFunctionType
+
+P = 128
+PACK = 4
+BATCH, SEQ, EMB = 4, 1024, 1024
+HEADS, NOPE, ROPE = 4, 64, 32
+HEAD = NOPE + ROPE
+RANK = 512
+PAIRS = ROPE // 2
+BASE = 10000.0
+
+TILES = 4
+ROUND = TILES * P
+ROUNDS = BATCH * SEQ // ROUND
+ROUNDS_PER_SEQ = SEQ // ROUND
+PASSES_1 = EMB // (P * PACK)
+RANK_TILES = RANK // P
+WORDS = EMB // 2
+PLAIN_COLS = HEADS * NOPE
+TURNED_COLS = HEADS * 2 * ROPE
+
+FLOPS = 2 * BATCH * SEQ * (EMB * RANK + RANK * HEADS * HEAD)
+
+TWO_PI = 2.0 * math.pi
+TWO_PI_HIGH = math.floor(TWO_PI * 8192.0) / 8192.0
+TWO_PI_LOW = TWO_PI - TWO_PI_HIGH
+PHASES = (0.5 * math.pi, math.pi, 0.0)
+
+
+def tile_multilatentattention_pa_t_kernel(tc, x, Wqa, Wqb, out):
+    nc = tc.nc
+    with ExitStack() as ctx:
+        keep = ctx.enter_context(tc.tile_pool(name="keep", bufs=1))
+        work = ctx.enter_context(tc.tile_pool(name="work", bufs=2))
+        psum = ctx.enter_context(tc.psum_pool(name="psum", bufs=1))
+        ctx.enter_context(tc.manual_schedule())
+
+        x_rounds = x.flatten_outer_dims().rearrange("(r p j) e -> r p (j e)", p=P, j=TILES)
+        x_sb = keep.tile([P, ROUNDS, TILES, EMB], BF16)
+        x_words = x_sb[:].bitcast(F32)
+        wa_raw = keep.tile([P, PASSES_1, PACK, RANK], BF16)
+        wb_raw = keep.tile([P, PACK, HEADS * HEAD], BF16)
+
+        def load_x(r):
+            nc.sync.dma_start(out=x_sb[:, r].rearrange("p j e -> p (j e)"), in_=x_rounds[r])
+
+        nc.sync.dma_start(
+            out=wa_raw[:].rearrange("p g (u e) c -> p (g u) (e c)", e=2),
+            in_=Wqa.rearrange("(a p e) c -> p a (e c)", p=P, e=2),
+        )
+        load_x(0)
+        load_x(1)
+        nc.sync.dma_start(out=wb_raw[:], in_=Wqb.rearrange("(t p) n -> p t n", p=P))
+        for r in range(2, ROUNDS):
+            load_x(r)
+
+        zero = keep.tile([P, 1], F32)
+        nc.gpsimd.memset(zero[:], 0.0)
+        warm = keep.tile([P, 1], F32)
+        nc.scalar.activation(out=warm[:], in_=zero[:], func=ACT.Sin)
+
+        classes = ROUNDS_PER_SEQ * TILES
+        position = keep.tile([P, classes], F32)
+        nc.gpsimd.iota(
+            position[:],
+            pattern=[[ROUND, ROUNDS_PER_SEQ], [1, TILES]],
+            base=0,
+            channel_multiplier=TILES,
+            allow_small_or_imprecise_dtypes=True,
+        )
+        ident = keep.tile([P, P], F32)
+        make_identity(nc, ident[:])
+
+        plain_angle = keep.tile([P, PAIRS, classes], F32)
+        for i in range(PAIRS):
+            nc.vector.tensor_scalar(
+                out=plain_angle[:, i, :],
+                in0=position[:],
+                scalar1=BASE ** (-float(i) / PAIRS),
+                scalar2=None,
+                op0=ALU.mult,
+            )
+        angle = keep.tile([P, len(PHASES), PAIRS, classes], F32)
+        for s in range(len(PHASES)):
+            nc.vector.tensor_scalar(
+                out=angle[:, s], in0=plain_angle[:], scalar1=PHASES[s], scalar2=None, op0=ALU.add
+            )
+        turns_int = keep.tile([P, len(PHASES), PAIRS, classes], I32)
+        nc.vector.tensor_scalar(
+            out=turns_int[:], in0=angle[:], scalar1=1.0 / TWO_PI, scalar2=None, op0=ALU.mult
+        )
+        turns = keep.tile([P, len(PHASES), PAIRS, classes], F32)
+        nc.vector.tensor_copy(out=turns[:], in_=turns_int[:])
+        for part in (TWO_PI_HIGH, TWO_PI_LOW):
+            nc.vector.scalar_tensor_tensor(
+                out=angle[:], in0=turns[:], scalar=-part, in1=angle[:], op0=ALU.mult, op1=ALU.add
+            )
+        wrap = keep.tile([P, len(PHASES), PAIRS, classes], F32)
+        nc.vector.tensor_scalar(
+            out=wrap[:], in0=angle[:], scalar1=math.pi, scalar2=-TWO_PI, op0=ALU.is_gt, op1=ALU.mult
+        )
+        nc.vector.tensor_tensor(out=angle[:], in0=angle[:], in1=wrap[:], op=ALU.add)
+        nc.vector.tensor_scalar(
+            out=wrap[:], in0=angle[:], scalar1=-math.pi, scalar2=TWO_PI, op0=ALU.is_lt, op1=ALU.mult
+        )
+        nc.vector.tensor_tensor(out=angle[:], in0=angle[:], in1=wrap[:], op=ALU.add)
+        factors = keep.tile([P, classes, 2, PAIRS, 2], F32)
+        nc.scalar.activation(
+            out=factors[:, :, 0],
+            in_=angle[:, 0].rearrange("p i c -> p c i").unsqueeze(3).to_broadcast([P, classes, PAIRS, 2]),
+            func=ACT.Sin,
+        )
+        nc.scalar.activation(
+            out=factors[:, :, 1], in_=angle[:, 1:3].rearrange("p s i c -> p c i s"), func=ACT.Sin
+        )
+
+        wa_grouped = keep.tile([P, PASSES_1, RANK, PACK], BF16, align_bytes=64)
+        for g in range(PASSES_1):
+            nc.vector.tensor_copy(
+                out=wa_grouped[:, g].rearrange("p (c i) t -> p c t i", i=4),
+                in_=wa_raw[:, g].rearrange("p t (c i) -> p c t i", i=4),
+            )
+        wa_codes = keep.tile([P, PASSES_1, RANK], U32, align_bytes=64)
+        wa_scales = keep.tile([P, PASSES_1, RANK], U8, align_bytes=64)
+        nc.vector.quantize_mx(
+            out=wa_codes[:].rearrange("p g c -> p (g c)").bitcast(FP8X4),
+            scales=wa_scales[:].rearrange("p g c -> p (g c)"),
+            in_=wa_grouped[:].rearrange("p g c t -> p (g c t)"),
+        )
+
+        wb_codes = keep.tile([P, PLAIN_COLS + TURNED_COLS], U32, align_bytes=64)
+        wb_scales = keep.tile([P, PLAIN_COLS + TURNED_COLS], U8, align_bytes=64)
+
+        def prepare_wb():
+            wb_grouped = keep.tile([P, PLAIN_COLS + TURNED_COLS, PACK], BF16, align_bytes=64)
+            by_head = wb_raw[:].rearrange("p t (h f) -> p h f t", f=HEAD)
+            nc.vector.tensor_copy(
+                out=wb_grouped[:, 0:PLAIN_COLS, :].rearrange("p (h f) t -> p h f t", f=NOPE),
+                in_=by_head[:, :, 0:NOPE, :],
+            )
+            turned = wb_grouped[:, PLAIN_COLS:, :].rearrange("p (h s f) t -> p h s f t", s=2, f=ROPE)
+            nc.vector.tensor_copy(out=turned[:, :, 0], in_=by_head[:, :, NOPE:HEAD, :])
+            swapped = turned[:, :, 1].rearrange("p h (i e) t -> p h i e t", e=2)
+            pairs = by_head[:, :, NOPE:HEAD, :].rearrange("p h (i e) t -> p h i e t", e=2)
+            for e in range(2):
+                nc.vector.tensor_copy(out=swapped[:, :, :, e, :], in_=pairs[:, :, :, 1 - e, :])
+            nc.vector.quantize_mx(
+                out=wb_codes[:].bitcast(FP8X4),
+                scales=wb_scales[:],
+                in_=wb_grouped[:].rearrange("p c t -> p (c t)"),
+            )
+
+        x_quantised = {}
+        cq_grouped = {}
+        cq_quantised = {}
+        results = {}
+
+        def transpose_x(r):
+            banks = []
+            for j in range(TILES):
+                xt = psum.tile([P, PASSES_1 * 2, P], F32, tag="xt", bufs=TILES)
+                for a in range(PASSES_1 * 2):
+                    nc.tensor.transpose(xt[:, a, :], x_words[:, r, j, a * P : (a + 1) * P], ident[:])
+                banks.append(xt)
+            x_grouped = work.tile([P, TILES, PASSES_1, P, PACK], BF16, align_bytes=64)
+            x_codes = work.tile([P, TILES, PASSES_1, P], U32, align_bytes=64)
+            x_scales = work.tile([P, TILES, PASSES_1, P], U8, align_bytes=64)
+            x_quantised[r] = (x_codes, x_scales, x_grouped)
+            for half in range(2):
+                for j in range(2 * half, 2 * half + 2):
+                    nc.scalar.copy(
+                        out=x_grouped[:, j].bitcast(F32),
+                        in_=banks[j][:].rearrange("p (g u) n -> p g n u", u=2),
+                    )
+                if half == 0:
+                    quantise_x(r, half)
+
+        def quantise_x(r, half):
+            x_codes, x_scales, x_grouped = x_quantised[r]
+            two = slice(2 * half, 2 * half + 2)
+            nc.vector.quantize_mx(
+                out=x_codes[:, two].rearrange("p j g n -> p (j g n)").bitcast(FP8X4),
+                scales=x_scales[:, two].rearrange("p j g n -> p (j g n)"),
+                in_=x_grouped[:, two].rearrange("p j g n t -> p (j g n t)"),
+            )
+
+        def first_product(r, half):
+            x_codes, x_scales, x_grouped = x_quantised[r]
+            if half == 0:
+                cq_bf = work.tile([P, TILES, P, PACK], BF16, align_bytes=64)
+                cq_grouped[r] = cq_bf
+            for j in range(2 * half, 2 * half + 2):
+                cq_ps = psum.tile([P, RANK_TILES, P], F32, tag="cq", bufs=2)
+                for t in range(RANK_TILES):
+                    for g in range(PASSES_1):
+                        nc.tensor.matmul_mx(
+                            out=cq_ps[:, t, :],
+                            lhsT=wa_codes[:, g, t * P : (t + 1) * P].bitcast(FP8X4),
+                            lhsT_scale=wa_scales[:, g, t * P : (t + 1) * P],
+                            rhs=x_codes[:, j, g, :].bitcast(FP8X4),
+                            rhs_scale=x_scales[:, j, g, :],
+                            start=(g == 0),
+                            stop=(g == PASSES_1 - 1),
+                        )
+                if j % 2 == 0:
+                    nc.scalar.copy(out=cq_grouped[r][:, j], in_=cq_ps[:].rearrange("p t n -> p n t"))
+                else:
+                    nc.vector.tensor_copy(out=cq_grouped[r][:, j], in_=cq_ps[:].rearrange("p t n -> p n t"))
+
+        def quantise_cq(r):
+            cq_codes = work.tile([P, TILES, P], U32, align_bytes=64)
+            cq_scales = work.tile([P, TILES, P], U8, align_bytes=64)
+            cq_quantised[r] = (cq_codes, cq_scales)
+            nc.vector.quantize_mx(
+                out=cq_codes[:].rearrange("p j n -> p (j n)").bitcast(FP8X4),
+                scales=cq_scales[:].rearrange("p j n -> p (j n)"),
+                in_=cq_grouped[r][:].rearrange("p j n t -> p (j n t)"),
+            )
+
+        def second_product(r, half):
+            cq_codes, cq_scales = cq_quantised[r]
+            if half == 0:
+                products = work.tile([P, TILES, HEADS, 2, ROPE], F32)
+                o_sb = work.tile([P, HEADS, TILES, HEAD], F32, bufs=3)
+                results[r] = (products, o_sb)
+            products, o_sb = results[r]
+            two = slice(2 * half, 2 * half + 2)
+            plain_ps = psum.tile([P, 2, PLAIN_COLS], F32, tag="plain", bufs=1)
+            turned_ps = psum.tile([P, 2, TURNED_COLS], F32, tag="turned", bufs=1)
+            for jj in range(2):
+                j = 2 * half + jj
+                for bank, cols in ((plain_ps, slice(0, PLAIN_COLS)), (turned_ps, slice(PLAIN_COLS, PLAIN_COLS + TURNED_COLS))):
+                    nc.tensor.matmul_mx(
+                        out=bank[:, jj, :],
+                        lhsT=cq_codes[:, j, :].bitcast(FP8X4),
+                        lhsT_scale=cq_scales[:, j, :],
+                        rhs=wb_codes[:, cols].bitcast(FP8X4),
+                        rhs_scale=wb_scales[:, cols],
+                        start=True,
+                        stop=True,
+                    )
+            nc.scalar.copy(
+                out=o_sb[:, :, two, 0:NOPE].rearrange("p h j f -> p j h f"),
+                in_=plain_ps[:].rearrange("p j (h f) -> p j h f", f=NOPE),
+            )
+            first_class = (r % ROUNDS_PER_SEQ) * TILES + 2 * half
+            nc.vector.tensor_tensor(
+                out=products[:, two].rearrange("p j h s f -> p j h (s f)"),
+                in0=turned_ps[:].rearrange("p j (h f) -> p j h f", f=2 * ROPE),
+                in1=factors[:, first_class : first_class + 2]
+                .rearrange("p c s i e -> p c (s i e)")
+                .unsqueeze(2)
+                .to_broadcast([P, 2, HEADS, 2 * ROPE]),
+                op=ALU.mult,
+            )
+
+        def finish(r):
+            products, o_sb = results[r]
+            nc.vector.tensor_tensor(
+                out=o_sb[:, :, :, NOPE:HEAD].rearrange("p h j f -> p j h f"),
+                in0=products[:, :, :, 0, :],
+                in1=products[:, :, :, 1, :],
+                op=ALU.add,
+            )
+            b = r // ROUNDS_PER_SEQ
+            n0 = (r % ROUNDS_PER_SEQ) * ROUND
+            nc.sync.dma_start(
+                out=out[b, :, n0 : n0 + ROUND, :].rearrange("h (p j) f -> p h (j f)", j=TILES),
+                in_=o_sb[:].rearrange("p h j f -> p h (j f)"),
+            )
+
+        for s in range(ROUNDS + 2):
+            if s < ROUNDS:
+                transpose_x(s)
+            for half in range(2):
+                if 0 <= s - 1 < ROUNDS:
+                    first_product(s - 1, half)
+                if 0 <= s - 2:
+                    second_product(s - 2, half)
+                if half == 0 and s < ROUNDS:
+                    quantise_x(s, 1)
+            if 0 <= s - 1 < ROUNDS:
+                quantise_cq(s - 1)
+            if 0 <= s - 2:
+                finish(s - 2)
+            if s == 1:
+                prepare_wb()

@@ -28,6 +28,7 @@ ROUNDS = BATCH * SEQ // ROUND
 ROUNDS_PER_SEQ = SEQ // ROUND
 PASSES_1 = EMB // (P * PACK)
 RANK_TILES = RANK // P
+BANKS = 8
 WORDS = EMB // 2
 PLAIN_COLS = HEADS * NOPE
 TURNED_COLS = HEADS * 2 * ROPE
@@ -163,6 +164,14 @@ def tile_multilatentattention_pa_t_kernel(tc, x, Wqa, Wqb, out):
                 in_=wb_grouped[:].rearrange("p c t -> p (c t)"),
             )
 
+        banks_taken = []
+
+        def next_bank(shape):
+            tag = "bank%d" % (len(banks_taken) % BANKS)
+            bank = psum.tile(shape, F32, name=tag, tag=tag)
+            banks_taken.append(tag)
+            return bank
+
         x_quantised = {}
         cq_grouped = {}
         cq_quantised = {}
@@ -171,7 +180,7 @@ def tile_multilatentattention_pa_t_kernel(tc, x, Wqa, Wqb, out):
         def transpose_x(r):
             banks = []
             for j in range(TILES):
-                xt = psum.tile([P, PASSES_1 * 2, P], F32, tag="xt", bufs=TILES)
+                xt = next_bank([P, PASSES_1 * 2, P])
                 for a in range(PASSES_1 * 2):
                     nc.tensor.transpose(xt[:, a, :], x_words[:, r, j, a * P : (a + 1) * P], ident[:])
                 banks.append(xt)
@@ -203,7 +212,7 @@ def tile_multilatentattention_pa_t_kernel(tc, x, Wqa, Wqb, out):
                 cq_bf = work.tile([P, TILES, P, PACK], BF16, align_bytes=64)
                 cq_grouped[r] = cq_bf
             for j in range(2 * half, 2 * half + 2):
-                cq_ps = psum.tile([P, RANK_TILES, P], F32, tag="cq", bufs=2)
+                cq_ps = next_bank([P, RANK_TILES, P])
                 for t in range(RANK_TILES):
                     for g in range(PASSES_1):
                         nc.tensor.matmul_mx(
@@ -220,14 +229,17 @@ def tile_multilatentattention_pa_t_kernel(tc, x, Wqa, Wqb, out):
                 else:
                     nc.vector.tensor_copy(out=cq_grouped[r][:, j], in_=cq_ps[:].rearrange("p t n -> p n t"))
 
-        def quantise_cq(r):
-            cq_codes = work.tile([P, TILES, P], U32, align_bytes=64)
-            cq_scales = work.tile([P, TILES, P], U8, align_bytes=64)
-            cq_quantised[r] = (cq_codes, cq_scales)
+        def quantise_cq(r, half):
+            if half == 0:
+                cq_codes = work.tile([P, TILES, P], U32, align_bytes=64)
+                cq_scales = work.tile([P, TILES, P], U8, align_bytes=64)
+                cq_quantised[r] = (cq_codes, cq_scales)
+            cq_codes, cq_scales = cq_quantised[r]
+            two = slice(2 * half, 2 * half + 2)
             nc.vector.quantize_mx(
-                out=cq_codes[:].rearrange("p j n -> p (j n)").bitcast(FP8X4),
-                scales=cq_scales[:].rearrange("p j n -> p (j n)"),
-                in_=cq_grouped[r][:].rearrange("p j n t -> p (j n t)"),
+                out=cq_codes[:, two].rearrange("p j n -> p (j n)").bitcast(FP8X4),
+                scales=cq_scales[:, two].rearrange("p j n -> p (j n)"),
+                in_=cq_grouped[r][:, two].rearrange("p j n t -> p (j n t)"),
             )
 
         def second_product(r, half):
@@ -238,8 +250,8 @@ def tile_multilatentattention_pa_t_kernel(tc, x, Wqa, Wqb, out):
                 results[r] = (products, o_sb)
             products, o_sb = results[r]
             two = slice(2 * half, 2 * half + 2)
-            plain_ps = psum.tile([P, 2, PLAIN_COLS], F32, tag="plain", bufs=1)
-            turned_ps = psum.tile([P, 2, TURNED_COLS], F32, tag="turned", bufs=1)
+            plain_ps = next_bank([P, 2, PLAIN_COLS])
+            turned_ps = next_bank([P, 2, TURNED_COLS])
             for jj in range(2):
                 j = 2 * half + jj
                 for bank, cols in ((plain_ps, slice(0, PLAIN_COLS)), (turned_ps, slice(PLAIN_COLS, PLAIN_COLS + TURNED_COLS))):
@@ -290,11 +302,11 @@ def tile_multilatentattention_pa_t_kernel(tc, x, Wqa, Wqb, out):
                     first_product(s - 1, half)
                 if 0 <= s - 2:
                     second_product(s - 2, half)
+                if 0 <= s - 1 < ROUNDS:
+                    quantise_cq(s - 1, half)
                 if half == 0 and s < ROUNDS:
                     quantise_x(s, 1)
-            if 0 <= s - 1 < ROUNDS:
-                quantise_cq(s - 1)
             if 0 <= s - 2:
                 finish(s - 2)
-            if s == 1:
+            if s == 0:
                 prepare_wb()

@@ -29,6 +29,7 @@ ROUNDS_PER_SEQ = SEQ // ROUND
 PASSES_1 = EMB // (P * PACK)
 RANK_TILES = RANK // P
 BANKS = 8
+VECTOR_TILE = 1
 WORDS = EMB // 2
 PLAIN_COLS = HEADS * NOPE
 TURNED_COLS = HEADS * 2 * ROPE
@@ -224,10 +225,10 @@ def tile_multilatentattention_pa_t_kernel(tc, x, Wqa, Wqb, out):
                             start=(g == 0),
                             stop=(g == PASSES_1 - 1),
                         )
-                if j % 2 == 0:
-                    nc.scalar.copy(out=cq_grouped[r][:, j], in_=cq_ps[:].rearrange("p t n -> p n t"))
-                else:
+                if j == VECTOR_TILE:
                     nc.vector.tensor_copy(out=cq_grouped[r][:, j], in_=cq_ps[:].rearrange("p t n -> p n t"))
+                else:
+                    nc.scalar.copy(out=cq_grouped[r][:, j], in_=cq_ps[:].rearrange("p t n -> p n t"))
 
         def quantise_cq(r, half):
             if half == 0:

@@ -280,19 +280,20 @@ def tile_multilatentattention_pa_t_kernel(tc, x, Wqa, Wqb, out):
                 op=ALU.mult,
             )
 
-        def finish(r):
+        def finish(r, half):
             products, o_sb = results[r]
+            two = slice(2 * half, 2 * half + 2)
             nc.vector.tensor_tensor(
-                out=o_sb[:, :, :, NOPE:HEAD].rearrange("p h j f -> p j h f"),
-                in0=products[:, :, :, 0, :],
-                in1=products[:, :, :, 1, :],
+                out=o_sb[:, :, two, NOPE:HEAD].rearrange("p h j f -> p j h f"),
+                in0=products[:, two, :, 0, :],
+                in1=products[:, two, :, 1, :],
                 op=ALU.add,
             )
             b = r // ROUNDS_PER_SEQ
             n0 = (r % ROUNDS_PER_SEQ) * ROUND
             nc.sync.dma_start(
-                out=out[b, :, n0 : n0 + ROUND, :].rearrange("h (p j) f -> p h (j f)", j=TILES),
-                in_=o_sb[:].rearrange("p h j f -> p h (j f)"),
+                out=out[b, :, n0 : n0 + ROUND, :].rearrange("h (p j) f -> p h j f", j=TILES)[:, :, two, :],
+                in_=o_sb[:, :, two, :],
             )
 
         for s in range(ROUNDS + 2):
@@ -305,9 +306,9 @@ def tile_multilatentattention_pa_t_kernel(tc, x, Wqa, Wqb, out):
                     second_product(s - 2, half)
                 if 0 <= s - 1 < ROUNDS:
                     quantise_cq(s - 1, half)
+                if 0 <= s - 2:
+                    finish(s - 2, half)
                 if half == 0 and s < ROUNDS:
                     quantise_x(s, 1)
-            if 0 <= s - 2:
-                finish(s - 2)
             if s == 0:
                 prepare_wb()

import math
from contextlib import ExitStack

import concourse.mybir as mybir
from concourse.masks import make_identity

F32 = mybir.dt.float32
BF16 = mybir.dt.bfloat16
I32 = mybir.dt.int32
U32 = mybir.dt.uint32
U8 = mybir.dt.uint8
FP8X4 = mybir.dt.float8_e4m3fn_x4
ALU = mybir.AluOpType
ACT = mybir.ActivationFunctionType

P = 128
PACK = 4
BATCH, SEQ, EMB = 4, 1024, 1024
HEADS, NOPE, ROPE = 4, 64, 32
HEAD = NOPE + ROPE
RANK = 512
PAIRS = ROPE // 2
BASE = 10000.0

TILES = 4
ROUND = TILES * P
ROUNDS = BATCH * SEQ // ROUND
ROUNDS_PER_SEQ = SEQ // ROUND
PASSES_1 = EMB // (P * PACK)
RANK_TILES = RANK // P
BANKS = 8
VECTOR_TILE = 1
WORDS = EMB // 2
PLAIN_COLS = HEADS * NOPE
TURNED_COLS = HEADS * 2 * ROPE

FLOPS = 2 * BATCH * SEQ * (EMB * RANK + RANK * HEADS * HEAD)

TWO_PI = 2.0 * math.pi
TWO_PI_HIGH = math.floor(TWO_PI * 8192.0) / 8192.0
TWO_PI_LOW = TWO_PI - TWO_PI_HIGH
PHASES = (0.5 * math.pi, math.pi, 0.0)


def tile_multilatentattention_pa_t_kernel(tc, x, Wqa, Wqb, out):
    nc = tc.nc
    with ExitStack() as ctx:
        keep = ctx.enter_context(tc.tile_pool(name="keep", bufs=1))
        work = ctx.enter_context(tc.tile_pool(name="work", bufs=2))
        psum = ctx.enter_context(tc.psum_pool(name="psum", bufs=1))
        ctx.enter_context(tc.manual_schedule())

        x_rounds = x.flatten_outer_dims().rearrange("(r p j) e -> r p (j e)", p=P, j=TILES)
        x_sb = keep.tile([P, ROUNDS, TILES, EMB], BF16)
        x_words = x_sb[:].bitcast(F32)
        wa_raw = keep.tile([P, PASSES_1, PACK, RANK], BF16)
        wb_raw = keep.tile([P, PACK, HEADS * HEAD], BF16)

        def load_x(r):
            nc.sync.dma_start(out=x_sb[:, r].rearrange("p j e -> p (j e)"), in_=x_rounds[r])

        nc.sync.dma_start(
            out=wa_raw[:].rearrange("p g (u e) c -> p (g u) (e c)", e=2),
            in_=Wqa.rearrange("(a p e) c -> p a (e c)", p=P, e=2),
        )
        load_x(0)
        load_x(1)
        nc.sync.dma_start(out=wb_raw[:], in_=Wqb.rearrange("(t p) n -> p t n", p=P))
        for r in range(2, ROUNDS):
            load_x(r)

        zero = keep.tile([P, 1], F32)
        nc.gpsimd.memset(zero[:], 0.0)
        warm = keep.tile([P, 1], F32)
        nc.scalar.activation(out=warm[:], in_=zero[:], func=ACT.Sin)

        classes = ROUNDS_PER_SEQ * TILES
        position = keep.tile([P, classes], F32)
        nc.gpsimd.iota(
            position[:],
            pattern=[[ROUND, ROUNDS_PER_SEQ], [1, TILES]],
            base=0,
            channel_multiplier=TILES,
            allow_small_or_imprecise_dtypes=True,
        )
        ident = keep.tile([P, P], F32)
        make_identity(nc, ident[:])

        plain_angle = keep.tile([P, PAIRS, classes], F32)
        for i in range(PAIRS):
            nc.vector.tensor_scalar(
                out=plain_angle[:, i, :],
                in0=position[:],
                scalar1=BASE ** (-float(i) / PAIRS),
                scalar2=None,
                op0=ALU.mult,
            )
        angle = keep.tile([P, len(PHASES), PAIRS, classes], F32)
        for s in range(len(PHASES)):
            nc.vector.tensor_scalar(
                out=angle[:, s], in0=plain_angle[:], scalar1=PHASES[s], scalar2=None, op0=ALU.add
            )
        turns_int = keep.tile([P, len(PHASES), PAIRS, classes], I32)
        nc.vector.tensor_scalar(
            out=turns_int[:], in0=angle[:], scalar1=1.0 / TWO_PI, scalar2=None, op0=ALU.mult
        )
        turns = keep.tile([P, len(PHASES), PAIRS, classes], F32)
        nc.vector.tensor_copy(out=turns[:], in_=turns_int[:])
        for part in (TWO_PI_HIGH, TWO_PI_LOW):
            nc.vector.scalar_tensor_tensor(
                out=angle[:], in0=turns[:], scalar=-part, in1=angle[:], op0=ALU.mult, op1=ALU.add
            )
        wrap = keep.tile([P, len(PHASES), PAIRS, classes], F32)
        nc.vector.tensor_scalar(
            out=wrap[:], in0=angle[:], scalar1=math.pi, scalar2=-TWO_PI, op0=ALU.is_gt, op1=ALU.mult
        )
        nc.vector.tensor_tensor(out=angle[:], in0=angle[:], in1=wrap[:], op=ALU.add)
        nc.vector.tensor_scalar(
            out=wrap[:], in0=angle[:], scalar1=-math.pi, scalar2=TWO_PI, op0=ALU.is_lt, op1=ALU.mult
        )
        nc.vector.tensor_tensor(out=angle[:], in0=angle[:], in1=wrap[:], op=ALU.add)
        factors = keep.tile([P, classes, 2, PAIRS, 2], F32)
        nc.scalar.activation(
            out=factors[:, :, 0],
            in_=angle[:, 0].rearrange("p i c -> p c i").unsqueeze(3).to_broadcast([P, classes, PAIRS, 2]),
            func=ACT.Sin,
        )
        nc.scalar.activation(
            out=factors[:, :, 1], in_=angle[:, 1:3].rearrange("p s i c -> p c i s"), func=ACT.Sin
        )

        wa_grouped = keep.tile([P, PASSES_1, RANK, PACK], BF16, align_bytes=64)
        for g in range(PASSES_1):
            nc.vector.tensor_copy(
                out=wa_grouped[:, g].rearrange("p (c i) t -> p c t i", i=4),
                in_=wa_raw[:, g].rearrange("p t (c i) -> p c t i", i=4),
            )
        wa_codes = keep.tile([P, PASSES_1, RANK], U32, align_bytes=64)
        wa_scales = keep.tile([P, PASSES_1, RANK], U8, align_bytes=64)
        nc.vector.quantize_mx(
            out=wa_codes[:].rearrange("p g c -> p (g c)").bitcast(FP8X4),
            scales=wa_scales[:].rearrange("p g c -> p (g c)"),
            in_=wa_grouped[:].rearrange("p g c t -> p (g c t)"),
        )

        wb_codes = keep.tile([P, PLAIN_COLS + TURNED_COLS], U32, align_bytes=64)
        wb_scales = keep.tile([P, PLAIN_COLS + TURNED_COLS], U8, align_bytes=64)

        def prepare_wb():
            wb_grouped = keep.tile([P, PLAIN_COLS + TURNED_COLS, PACK], BF16, align_bytes=64)
            by_head = wb_raw[:].rearrange("p t (h f) -> p h f t", f=HEAD)
            nc.vector.tensor_copy(
                out=wb_grouped[:, 0:PLAIN_COLS, :].rearrange("p (h f) t -> p h f t", f=NOPE),
                in_=by_head[:, :, 0:NOPE, :],
            )
            turned = wb_grouped[:, PLAIN_COLS:, :].rearrange("p (h s f) t -> p h s f t", s=2, f=ROPE)
            nc.vector.tensor_copy(out=turned[:, :, 0], in_=by_head[:, :, NOPE:HEAD, :])
            swapped = turned[:, :, 1].rearrange("p h (i e) t -> p h i e t", e=2)
            pairs = by_head[:, :, NOPE:HEAD, :].rearrange("p h (i e) t -> p h i e t", e=2)
            for e in range(2):
                nc.vector.tensor_copy(out=swapped[:, :, :, e, :], in_=pairs[:, :, :, 1 - e, :])
            nc.vector.quantize_mx(
                out=wb_codes[:].bitcast(FP8X4),
                scales=wb_scales[:],
                in_=wb_grouped[:].rearrange("p c t -> p (c t)"),
            )

        banks_taken = []

        def next_bank(shape):
            tag = "bank%d" % (len(banks_taken) % BANKS)
            bank = psum.tile(shape, F32, name=tag, tag=tag)
            banks_taken.append(tag)
            return bank

        x_quantised = {}
        cq_grouped = {}
        cq_quantised = {}
        results = {}

        def transpose_x(r):
            banks = []
            for j in range(TILES):
                xt = next_bank([P, PASSES_1 * 2, P])
                for a in range(PASSES_1 * 2):
                    nc.tensor.transpose(xt[:, a, :], x_words[:, r, j, a * P : (a + 1) * P], ident[:])
                banks.append(xt)
            x_grouped = work.tile([P, TILES, PASSES_1, P, PACK], BF16, align_bytes=64)
            x_codes = work.tile([P, TILES, PASSES_1, P], U32, align_bytes=64)
            x_scales = work.tile([P, TILES, PASSES_1, P], U8, align_bytes=64)
            x_quantised[r] = (x_codes, x_scales, x_grouped)
            for half in range(2):
                for j in range(2 * half, 2 * half + 2):
                    nc.scalar.copy(
                        out=x_grouped[:, j].bitcast(F32),
                        in_=banks[j][:].rearrange("p (g u) n -> p g n u", u=2),
                    )
                if half == 0:
                    quantise_x(r, half)

        def quantise_x(r, half):
            x_codes, x_scales, x_grouped = x_quantised[r]
            two = slice(2 * half, 2 * half + 2)
            nc.vector.quantize_mx(
                out=x_codes[:, two].rearrange("p j g n -> p (j g n)").bitcast(FP8X4),
                scales=x_scales[:, two].rearrange("p j g n -> p (j g n)"),
                in_=x_grouped[:, two].rearrange("p j g n t -> p (j g n t)"),
            )

        def first_product(r, half):
            x_codes, x_scales, x_grouped = x_quantised[r]
            if half == 0:
                cq_bf = work.tile([P, TILES, P, PACK], BF16, align_bytes=64)
                cq_grouped[r] = cq_bf
            for j in range(2 * half, 2 * half + 2):
                cq_ps = next_bank([P, RANK_TILES, P])
                for t in range(RANK_TILES):
                    for g in range(PASSES_1):
                        nc.tensor.matmul_mx(
                            out=cq_ps[:, t, :],
                            lhsT=wa_codes[:, g, t * P : (t + 1) * P].bitcast(FP8X4),
                            lhsT_scale=wa_scales[:, g, t * P : (t + 1) * P],
                            rhs=x_codes[:, j, g, :].bitcast(FP8X4),
                            rhs_scale=x_scales[:, j, g, :],
                            start=(g == 0),
                            stop=(g == PASSES_1 - 1),
                        )
                if j == VECTOR_TILE:
                    nc.vector.tensor_copy(out=cq_grouped[r][:, j], in_=cq_ps[:].rearrange("p t n -> p n t"))
                else:
                    nc.scalar.copy(out=cq_grouped[r][:, j], in_=cq_ps[:].rearrange("p t n -> p n t"))

        def quantise_cq(r, half):
            if half == 0:
                cq_codes = work.tile([P, TILES, P], U32, align_bytes=64)
                cq_scales = work.tile([P, TILES, P], U8, align_bytes=64)
                cq_quantised[r] = (cq_codes, cq_scales)
            cq_codes, cq_scales = cq_quantised[r]
            two = slice(2 * half, 2 * half + 2)
            nc.vector.quantize_mx(
                out=cq_codes[:, two].rearrange("p j n -> p (j n)").bitcast(FP8X4),
                scales=cq_scales[:, two].rearrange("p j n -> p (j n)"),
                in_=cq_grouped[r][:, two].rearrange("p j n t -> p (j n t)"),
            )

        def second_product(r, half):
            cq_codes, cq_scales = cq_quantised[r]
            if half == 0:
                products = work.tile([P, TILES, HEADS, 2, ROPE], F32)
                o_sb = work.tile([P, HEADS, TILES, HEAD], F32, bufs=3)
                results[r] = (products, o_sb)
            products, o_sb = results[r]
            two = slice(2 * half, 2 * half + 2)
            plain_ps = next_bank([P, 2, PLAIN_COLS])
            turned_ps = next_bank([P, 2, TURNED_COLS])
            for jj in range(2):
                j = 2 * half + jj
                for bank, cols in ((plain_ps, slice(0, PLAIN_COLS)), (turned_ps, slice(PLAIN_COLS, PLAIN_COLS + TURNED_COLS))):
                    nc.tensor.matmul_mx(
                        out=bank[:, jj, :],
                        lhsT=cq_codes[:, j, :].bitcast(FP8X4),
                        lhsT_scale=cq_scales[:, j, :],
                        rhs=wb_codes[:, cols].bitcast(FP8X4),
                        rhs_scale=wb_scales[:, cols],
                        start=True,
                        stop=True,
                    )
            nc.scalar.copy(
                out=o_sb[:, :, two, 0:NOPE].rearrange("p h j f -> p j h f"),
                in_=plain_ps[:].rearrange("p j (h f) -> p j h f", f=NOPE),
            )
            first_class = (r % ROUNDS_PER_SEQ) * TILES + 2 * half
            nc.vector.tensor_tensor(
                out=products[:, two].rearrange("p j h s f -> p j h (s f)"),
                in0=turned_ps[:].rearrange("p j (h f) -> p j h f", f=2 * ROPE),
                in1=factors[:, first_class : first_class + 2]
                .rearrange("p c s i e -> p c (s i e)")
                .unsqueeze(2)
                .to_broadcast([P, 2, HEADS, 2 * ROPE]),
                op=ALU.mult,
            )

        def finish(r, half):
            products, o_sb = results[r]
            two = slice(2 * half, 2 * half + 2)
            nc.vector.tensor_tensor(
                out=o_sb[:, :, two, NOPE:HEAD].rearrange("p h j f -> p j h f"),
                in0=products[:, two, :, 0, :],
                in1=products[:, two, :, 1, :],
                op=ALU.add,
            )
            b = r // ROUNDS_PER_SEQ
            n0 = (r % ROUNDS_PER_SEQ) * ROUND
            nc.sync.dma_start(
                out=out[b, :, n0 : n0 + ROUND, :].rearrange("h (p j) f -> p h j f", j=TILES)[:, :, two, :],
                in_=o_sb[:, :, two, :],
            )

        for s in range(ROUNDS + 2):
            if s < ROUNDS:
                transpose_x(s)
            for half in range(2):
                if 0 <= s - 1 < ROUNDS:
                    first_product(s - 1, half)
                if 0 <= s - 2:
                    second_product(s - 2, half)
                if 0 <= s - 1 < ROUNDS:
                    quantise_cq(s - 1, half)
                if 0 <= s - 2:
                    finish(s - 2, half)
                if half == 0 and s < ROUNDS:
                    quantise_x(s, 1)
            if s == 0:
                prepare_wb()
